import numpy as np
import ml_dtypes


def mxq(x, axis, fmt="e4m3"):
    dtype, down = {"e4m3": (ml_dtypes.float8_e4m3fn, 7), "e5m2": (ml_dtypes.float8_e5m2, 14)}[fmt]
    v = np.moveaxis(np.asarray(x, np.float32).astype(ml_dtypes.bfloat16).astype(np.float64), axis, -1)
    blocks = v.reshape(v.shape[:-1] + (-1, 32))
    amax = np.abs(blocks).max(-1, keepdims=True)
    byte = np.maximum(np.where(amax > 0, np.frexp(amax)[1] - 1 + 127, 0) - down, 1)
    scale = np.exp2(byte - 127.0)
    codes = (blocks / scale).astype(np.float32).astype(dtype).astype(np.float64)
    return np.moveaxis((codes * scale).reshape(v.shape), -1, axis)


WIDE = False


def mx_kscale(k):
    if not WIDE:
        return np.ones(k)
    levels = np.array([10, -10, 5, -5, 0])
    if k % 512:
        return np.exp2(np.random.permutation(np.resize(levels, k // 32))).repeat(32)
    a = np.empty((k // 512, 16))
    for p in range(k // 512):
        a[p, :8] = np.random.permutation(np.resize(levels, 8))
        for g in range(8):
            far = levels[np.abs(levels - a[p, g]) >= 10]
            a[p, g + 8] = far[np.random.randint(len(far))]
    return np.exp2(a.ravel()).repeat(32)


BF16 = ml_dtypes.bfloat16


def bf(x):
    return np.asarray(x, np.float32).astype(BF16)


def f64(x):
    return np.asarray(x).astype(np.float64)


B, D0, D1, D2, D3, D4 = 128, 512, 1024, 512, 1024, 256
DENSITY = 0.02


def setup_inputs():
    s, t = mx_kscale(D0), mx_kscale(D1)
    bound0 = np.sqrt(3.0 / (DENSITY * D0))
    bound1 = np.sqrt(6.0 / (DENSITY * D1))
    return {"x": bf(np.random.standard_normal((B, D0)) * s),
            "W0": bf(np.random.uniform(-bound0, bound0, (D1, D0)) / s[None, :] * t[:, None]),
            "b0": bf(np.random.standard_normal(D1) * 0.3 * t),
            "m0": bf(np.random.uniform(size=(D1, D0)) < DENSITY),
            "W1": bf(np.random.uniform(-bound1, bound1, (D2, D1)) / t[None, :]),
            "b1": bf(np.random.standard_normal(D2) * 0.3),
            "m1": bf(np.random.uniform(size=(D2, D1)) < DENSITY)}


def reference(x, W0, b0, m0, W1, b1, m1):
    h = f64(x).reshape(x.shape[0], -1)
    w0 = f64(W0) * f64(m0)
    pre0 = (mxq(h, 1, "e4m3") @ mxq(w0, 1, "e4m3").T) + f64(b0)
    h0 = np.maximum(pre0, 0.0)
    w1 = f64(W1) * f64(m1)
    pre1 = (mxq(h0, 1, "e4m3") @ mxq(w1, 1, "e4m3").T) + f64(b1)
    return np.maximum(pre1, 0.0)

@@ -1,0 +1,219 @@
+from contextlib import ExitStack
+
+import concourse.mybir as mybir
+from concourse.masks import make_identity
+
+BF16 = mybir.dt.bfloat16
+F32 = mybir.dt.float32
+U32 = mybir.dt.uint32
+U8 = mybir.dt.uint8
+FP8X4 = mybir.dt.float8_e4m3fn_x4
+RELU = mybir.ActivationFunctionType.Relu
+
+P = 128
+PACK = 4
+K_PASS = P * PACK
+HALVES = 2
+D0, D1, D2 = 512, 1024, 512
+FLOPS = 2 * P * (D0 * D1 + D1 * D2)
+
+SETS = 2
+CHUNK = SETS * K_PASS
+CHUNKS_0 = D1 * D0 // (P * CHUNK)
+CHUNKS_1 = D2 * D1 // (P * CHUNK)
+CHUNKS = CHUNKS_0 + CHUNKS_1
+PASSES_1 = D1 // K_PASS
+LAG = 2
+
+
+def tile_patchedsparsenetwork_pa_s_kernel(tc, x, W0, b0, m0, W1, b1, m1, out):
+    nc = tc.nc
+    with ExitStack() as ctx:
+        ctx.enter_context(tc.manual_schedule())
+        consts = ctx.enter_context(tc.tile_pool(name="consts", bufs=1))
+        keep = ctx.enter_context(tc.tile_pool(name="keep", bufs=1))
+        pieces = {c: [(0, SETS)] for c in range(CHUNKS)}
+        pieces[CHUNKS - 1] = [(s, 1) for s in range(SETS)]
+        stream = ctx.enter_context(tc.tile_pool(name="stream", bufs=CHUNKS + 1))
+        flip_psum = ctx.enter_context(tc.psum_pool(name="flip_psum", bufs=4))
+        sum_psum = ctx.enter_context(tc.psum_pool(name="sum_psum", bufs=4))
+
+        x_rows = consts.tile([P, D0], BF16)
+        nc.sync.dma_start(out=x_rows[:], in_=x)
+        b0_rows = consts.tile([P, K_PASS], BF16)
+        nc.vector.memset(b0_rows[:], 0.0)
+        nc.sync.dma_start(
+            out=b0_rows[0:PASSES_1, :], in_=b0.rearrange("(j n) -> j n", j=PASSES_1)
+        )
+        b1_rows = consts.tile([P, D2], BF16)
+        nc.vector.memset(b1_rows[:], 0.0)
+        nc.sync.dma_start(out=b1_rows[0:1, :], in_=b1.rearrange("(o n) -> o n", o=1))
+        deal = "(g q j e) k -> g j q (e k)"
+        w_dealt = W0.rearrange(deal, g=PASSES_1, q=P, e=SETS)
+        m_dealt = m0.rearrange(deal, g=PASSES_1, q=P, e=SETS)
+        w_views = [w_dealt[c // 2, c % 2] for c in range(CHUNKS_0)]
+        m_views = [m_dealt[c // 2, c % 2] for c in range(CHUNKS_0)]
+        w_views += [W1.rearrange("(r q) k -> r q k", q=P)[r] for r in range(CHUNKS_1)]
+        m_views += [m1.rearrange("(r q) k -> r q k", q=P)[r] for r in range(CHUNKS_1)]
+        w_rows, m_rows = [], []
+        for c in range(CHUNKS):
+            w_rows.append(stream.tile([P, CHUNK], BF16, name="w_rows"))
+            m_rows.append(stream.tile([P, CHUNK], BF16, name="m_rows"))
+            for first, sets in pieces[c]:
+                cols = slice(first * K_PASS, (first + sets) * K_PASS)
+                nc.sync.dma_start(out=w_rows[c][:, cols], in_=w_views[c][:, cols])
+                nc.sync.dma_start(out=m_rows[c][:, cols], in_=m_views[c][:, cols])
+
+        ident = consts.tile([P, P], F32)
+        make_identity(nc, ident[:])
+        ones = consts.tile([P, P], BF16)
+        nc.vector.memset(ones[:], 1.0)
+
+        x_codes = keep.tile([P, P], U32, align_bytes=64)
+        x_scales = keep.tile([P, P], U8, align_bytes=64)
+        w_codes = keep.tile([P, CHUNKS, SETS * P], U32, align_bytes=64)
+        w_scales = keep.tile([P, CHUNKS, SETS * P], U8, align_bytes=64)
+        h_codes = keep.tile([P, PASSES_1, P], U32, align_bytes=64)
+        h_scales = keep.tile([P, PASSES_1, P], U8, align_bytes=64)
+        h_tiles = keep.tile([P, PASSES_1, PACK, P], BF16)
+        h_grouped = keep.tile([P, PASSES_1, P, PACK], BF16, align_bytes=64)
+        out_sb = keep.tile([P, D2], F32)
+
+        def flip(rows, sets):
+            words = rows.bitcast(F32)
+            bank = flip_psum.tile([P, D2], F32, tag="bank")
+            for block in range(sets * HALVES):
+                s, h = divmod(block, HALVES)
+                nc.tensor.transpose(
+                    out=bank[:, block * P : (block + 1) * P],
+                    in_=words[:, s * HALVES * P + h : (s + 1) * HALVES * P : HALVES],
+                    identity=ident[:],
+                )
+            grouped = stream.tile([P, sets * P * PACK], BF16, name="grouped", align_bytes=64)
+            nc.scalar.copy(
+                out=grouped[:].bitcast(F32).rearrange("q (s n h) -> q s n h", s=sets, h=HALVES),
+                in_=bank[:, 0 : sets * HALVES * P].rearrange(
+                    "q (s h n) -> q s n h", s=sets, h=HALVES
+                ),
+            )
+            return grouped
+
+        x_grouped = flip(x_rows[:], 1)
+
+        b0_bank = flip_psum.tile([P, D2], F32, tag="bank")
+        for h in range(HALVES):
+            nc.tensor.transpose(
+                out=b0_bank[:, h * P : (h + 1) * P],
+                in_=b0_rows[:].bitcast(F32)[:, h : HALVES * P : HALVES],
+                identity=ident[:],
+            )
+        b0_cols = consts.tile([P, PASSES_1 * PACK], BF16)
+        nc.scalar.copy(
+            out=b0_cols[:].bitcast(F32).rearrange("q (j h) -> q j h", h=HALVES),
+            in_=b0_bank[:, 0 : HALVES * P].rearrange("q (h n) -> q n h", h=HALVES)[:, 0:PASSES_1, :],
+        )
+
+        b1_bank = flip_psum.tile([P, D2], F32, tag="bank")
+        nc.tensor.matmul(out=b1_bank[:], lhsT=ones[:], rhs=b1_rows[:], start=True, stop=True)
+        b1_all = consts.tile([P, D2], F32)
+        nc.scalar.copy(out=b1_all[:], in_=b1_bank[:])
+
+        grouped_of = {}
+        out_banks = {}
+
+        def front(c):
+            masked = stream.tile([P, CHUNK], BF16, name="masked")
+            for first, sets in pieces[c]:
+                cols = slice(first * K_PASS, (first + sets) * K_PASS)
+                nc.vector.tensor_mul(
+                    out=masked[:, cols], in0=w_rows[c][:, cols], in1=m_rows[c][:, cols]
+                )
+                grouped_of[c, first] = flip(masked[:, cols], sets)
+
+        def quantise(c):
+            for first, sets in pieces[c]:
+                cols = slice(first * P, (first + sets) * P)
+                nc.vector.quantize_mx(
+                    out=w_codes[:, c, cols].bitcast(FP8X4),
+                    scales=w_scales[:, c, cols],
+                    in_=grouped_of[c, first][:],
+                )
+
+        def multiply_0(c):
+            h_bank = sum_psum.tile([P, SETS, P], F32, tag="sum")
+            for e in range(SETS):
+                cols = slice(e * P, (e + 1) * P)
+                nc.tensor.matmul_mx(
+                    out=h_bank[:, e, :],
+                    lhsT=w_codes[:, c, cols].bitcast(FP8X4),
+                    lhsT_scale=w_scales[:, c, cols],
+                    rhs=x_codes[:].bitcast(FP8X4),
+                    rhs_scale=x_scales[:],
+                    start=True,
+                    stop=True,
+                )
+            for e in range(SETS):
+                pas, t = divmod(SETS * c + e, PACK)
+                nc.scalar.activation(
+                    out=h_tiles[:, pas, t, :],
+                    in_=h_bank[:, e, :],
+                    func=RELU,
+                    bias=b0_cols[:, SETS * c + e : SETS * c + e + 1],
+                )
+
+        def group_h(pas):
+            nc.vector.tensor_copy(
+                out=h_grouped[:, pas, :, :], in_=h_tiles[:, pas, :, :].rearrange("q t b -> q b t")
+            )
+
+        def quantise_h(pas):
+            nc.vector.quantize_mx(
+                out=h_codes[:, pas, :].bitcast(FP8X4),
+                scales=h_scales[:, pas, :],
+                in_=h_grouped[:, pas, :, :].rearrange("q b t -> q (b t)"),
+            )
+
+        def multiply_1(c):
+            out_banks[c] = sum_psum.tile([P, P], F32, name="out_bank", tag="sum")
+            for pas in range(PASSES_1):
+                cols = slice(pas * P, (pas + 1) * P)
+                nc.tensor.matmul_mx(
+                    out=out_banks[c][:],
+                    lhsT=h_codes[:, pas, :].bitcast(FP8X4),
+                    lhsT_scale=h_scales[:, pas, :],
+                    rhs=w_codes[:, c, cols].bitcast(FP8X4),
+                    rhs_scale=w_scales[:, c, cols],
+                    start=(pas == 0),
+                    stop=(pas == PASSES_1 - 1),
+                )
+
+        def finish_out(c):
+            cols = slice((c - CHUNKS_0) * P, (c - CHUNKS_0 + 1) * P)
+            nc.vector.tensor_add(out=out_sb[:, cols], in0=out_banks[c][:], in1=b1_all[:, cols])
+            nc.vector.tensor_scalar_max(out=out_sb[:, cols], in0=out_sb[:, cols], scalar1=0.0)
+            nc.sync.dma_start(out=out[:, cols], in_=out_sb[:, cols])
+
+        layer_0 = range(CHUNKS_0)
+        layer_1 = range(CHUNKS_0, CHUNKS)
+        h_done = CHUNKS_0 - 1 + 2 * LAG
+        multiply_step = {c: max(c + LAG, h_done) for c in layer_1}
+        for i in range(CHUNKS + 2 * LAG):
+            if i < CHUNKS:
+                front(i)
+            if i == 0:
+                nc.vector.quantize_mx(
+                    out=x_codes[:].bitcast(FP8X4), scales=x_scales[:], in_=x_grouped[:]
+                )
+            if 0 <= i - LAG < CHUNKS:
+                quantise(i - LAG)
+            if i - 2 * LAG in layer_0 and (i - 2 * LAG) % HALVES == HALVES - 1:
+                group_h((i - 2 * LAG) // HALVES)
+                quantise_h((i - 2 * LAG) // HALVES)
+            for c in layer_1:
+                if i == multiply_step[c] + LAG:
+                    finish_out(c)
+            if i - LAG in layer_0:
+                multiply_0(i - LAG)
+            for c in layer_1:
+                if i == multiply_step[c]:
+                    multiply_1(c)

@@ -11,6 +11,7 @@ FP8X4 = mybir.dt.float8_e4m3fn_x4
 RELU = mybir.ActivationFunctionType.Relu
 
 P = 128
+PAIR = 2
 PACK = 4
 K_PASS = P * PACK
 HALVES = 2
@@ -79,14 +80,18 @@ def tile_patchedsparsenetwork_pa_s_kernel(tc, x, W0, b0, m0, W1, b1, m1, out):
         h_grouped = keep.tile([P, PASSES_1, P, PACK], BF16, align_bytes=64)
         out_sb = keep.tile([P, D2], F32)
 
-        def flip(rows, sets):
+        def flip(rows, sets, parted):
             words = rows.bitcast(F32)
             bank = flip_psum.tile([P, D2], F32, tag="bank")
             for block in range(sets * HALVES):
                 s, h = divmod(block, HALVES)
+                if parted:
+                    in_cols = slice((h * sets + s) * P, (h * sets + s + 1) * P)
+                else:
+                    in_cols = slice(s * HALVES * P + h, (s + 1) * HALVES * P, HALVES)
                 nc.tensor.transpose(
                     out=bank[:, block * P : (block + 1) * P],
-                    in_=words[:, s * HALVES * P + h : (s + 1) * HALVES * P : HALVES],
+                    in_=words[:, in_cols],
                     identity=ident[:],
                 )
             grouped = stream.tile([P, sets * P * PACK], BF16, name="grouped", align_bytes=64)
@@ -98,7 +103,7 @@ def tile_patchedsparsenetwork_pa_s_kernel(tc, x, W0, b0, m0, W1, b1, m1, out):
             )
             return grouped
 
-        x_grouped = flip(x_rows[:], 1)
+        x_grouped = flip(x_rows[:], 1, False)
 
         b0_bank = flip_psum.tile([P, D2], F32, tag="bank")
         for h in range(HALVES):
@@ -125,10 +130,14 @@ def tile_patchedsparsenetwork_pa_s_kernel(tc, x, W0, b0, m0, W1, b1, m1, out):
             masked = stream.tile([P, CHUNK], BF16, name="masked")
             for first, sets in pieces[c]:
                 cols = slice(first * K_PASS, (first + sets) * K_PASS)
+                as_read = "q (n h e) -> q h n e"
+                as_written = "q (h n e) -> q h n e"
                 nc.vector.tensor_mul(
-                    out=masked[:, cols], in0=w_rows[c][:, cols], in1=m_rows[c][:, cols]
+                    out=masked[:, cols].rearrange(as_written, h=HALVES, e=PAIR),
+                    in0=w_rows[c][:, cols].rearrange(as_read, h=HALVES, e=PAIR),
+                    in1=m_rows[c][:, cols].rearrange(as_read, h=HALVES, e=PAIR),
                 )
-                grouped_of[c, first] = flip(masked[:, cols], sets)
+                grouped_of[c, first] = flip(masked[:, cols], sets, True)
 
         def quantise(c):
             for first, sets in pieces[c]:

@@ -19,12 +19,18 @@ D0, D1, D2 = 512, 1024, 512
 FLOPS = 2 * P * (D0 * D1 + D1 * D2)
 
 SETS = 2
-CHUNK = SETS * K_PASS
-CHUNKS_0 = D1 * D0 // (P * CHUNK)
-CHUNKS_1 = D2 * D1 // (P * CHUNK)
-CHUNKS = CHUNKS_0 + CHUNKS_1
 PASSES_1 = D1 // K_PASS
+CHUNKS_0 = D1 // (P * SETS)
+CHUNKS_1 = D2 // P
+CHUNKS = CHUNKS_0 + CHUNKS_1
 LAG = 2
+
+CUT = (0, CHUNKS - 1)
+PIECES = [
+    (c, first, 1 if c in CUT else SETS)
+    for c in range(CHUNKS)
+    for first in (range(SETS) if c in CUT else (0,))
+]
 
 
 def tile_patchedsparsenetwork_pa_s_kernel(tc, x, W0, b0, m0, W1, b1, m1, out):
@@ -33,22 +39,10 @@ def tile_patchedsparsenetwork_pa_s_kernel(tc, x, W0, b0, m0, W1, b1, m1, out):
         ctx.enter_context(tc.manual_schedule())
         consts = ctx.enter_context(tc.tile_pool(name="consts", bufs=1))
         keep = ctx.enter_context(tc.tile_pool(name="keep", bufs=1))
-        pieces = {c: [(0, SETS)] for c in range(CHUNKS)}
-        pieces[CHUNKS - 1] = [(s, 1) for s in range(SETS)]
-        stream = ctx.enter_context(tc.tile_pool(name="stream", bufs=CHUNKS + 1))
+        stream = ctx.enter_context(tc.tile_pool(name="stream", bufs=len(PIECES)))
         flip_psum = ctx.enter_context(tc.psum_pool(name="flip_psum", bufs=4))
         sum_psum = ctx.enter_context(tc.psum_pool(name="sum_psum", bufs=4))
 
-        x_rows = consts.tile([P, D0], BF16)
-        nc.sync.dma_start(out=x_rows[:], in_=x)
-        b0_rows = consts.tile([P, K_PASS], BF16)
-        nc.vector.memset(b0_rows[:], 0.0)
-        nc.sync.dma_start(
-            out=b0_rows[0:PASSES_1, :], in_=b0.rearrange("(j n) -> j n", j=PASSES_1)
-        )
-        b1_rows = consts.tile([P, D2], BF16)
-        nc.vector.memset(b1_rows[:], 0.0)
-        nc.sync.dma_start(out=b1_rows[0:1, :], in_=b1.rearrange("(o n) -> o n", o=1))
         deal = "(g q j e) k -> g j q (e k)"
         w_dealt = W0.rearrange(deal, g=PASSES_1, q=P, e=SETS)
         m_dealt = m0.rearrange(deal, g=PASSES_1, q=P, e=SETS)
@@ -56,14 +50,25 @@ def tile_patchedsparsenetwork_pa_s_kernel(tc, x, W0, b0, m0, W1, b1, m1, out):
         m_views = [m_dealt[c // 2, c % 2] for c in range(CHUNKS_0)]
         w_views += [W1.rearrange("(r q) k -> r q k", q=P)[r] for r in range(CHUNKS_1)]
         m_views += [m1.rearrange("(r q) k -> r q k", q=P)[r] for r in range(CHUNKS_1)]
+        x_rows = consts.tile([P, D0], BF16)
         w_rows, m_rows = [], []
-        for c in range(CHUNKS):
-            w_rows.append(stream.tile([P, CHUNK], BF16, name="w_rows"))
-            m_rows.append(stream.tile([P, CHUNK], BF16, name="m_rows"))
-            for first, sets in pieces[c]:
-                cols = slice(first * K_PASS, (first + sets) * K_PASS)
-                nc.sync.dma_start(out=w_rows[c][:, cols], in_=w_views[c][:, cols])
-                nc.sync.dma_start(out=m_rows[c][:, cols], in_=m_views[c][:, cols])
+        for i, (c, first, sets) in enumerate(PIECES):
+            cols = slice(first * K_PASS, (first + sets) * K_PASS)
+            w_rows.append(stream.tile([P, sets * K_PASS], BF16, name="w_rows"))
+            m_rows.append(stream.tile([P, sets * K_PASS], BF16, name="m_rows"))
+            nc.sync.dma_start(out=w_rows[i][:], in_=w_views[c][:, cols])
+            nc.sync.dma_start(out=m_rows[i][:], in_=m_views[c][:, cols])
+            if i == 0:
+                nc.sync.dma_start(out=x_rows[:], in_=x)
+
+        b0_rows = consts.tile([P, K_PASS], BF16)
+        nc.vector.memset(b0_rows[:], 0.0)
+        nc.gpsimd.dma_start(
+            out=b0_rows[0:PASSES_1, :], in_=b0.rearrange("(j n) -> j n", j=PASSES_1)
+        )
+        b1_rows = consts.tile([P, D2], BF16)
+        nc.vector.memset(b1_rows[:], 0.0)
+        nc.gpsimd.dma_start(out=b1_rows[0:1, :], in_=b1.rearrange("(o n) -> o n", o=1))
 
         ident = consts.tile([P, P], F32)
         make_identity(nc, ident[:])
@@ -103,54 +108,63 @@ def tile_patchedsparsenetwork_pa_s_kernel(tc, x, W0, b0, m0, W1, b1, m1, out):
             )
             return grouped
 
-        x_grouped = flip(x_rows[:], 1, False)
+        def flip_x():
+            return flip(x_rows[:], 1, False)
 
-        b0_bank = flip_psum.tile([P, D2], F32, tag="bank")
-        for h in range(HALVES):
-            nc.tensor.transpose(
-                out=b0_bank[:, h * P : (h + 1) * P],
-                in_=b0_rows[:].bitcast(F32)[:, h : HALVES * P : HALVES],
-                identity=ident[:],
+        def quantise_x(x_grouped):
+            nc.vector.quantize_mx(
+                out=x_codes[:].bitcast(FP8X4), scales=x_scales[:], in_=x_grouped[:]
             )
-        b0_cols = consts.tile([P, PASSES_1 * PACK], BF16)
-        nc.scalar.copy(
-            out=b0_cols[:].bitcast(F32).rearrange("q (j h) -> q j h", h=HALVES),
-            in_=b0_bank[:, 0 : HALVES * P].rearrange("q (h n) -> q n h", h=HALVES)[:, 0:PASSES_1, :],
-        )
 
-        b1_bank = flip_psum.tile([P, D2], F32, tag="bank")
-        nc.tensor.matmul(out=b1_bank[:], lhsT=ones[:], rhs=b1_rows[:], start=True, stop=True)
+        b0_cols = consts.tile([P, PASSES_1 * PACK], BF16)
         b1_all = consts.tile([P, D2], F32)
-        nc.scalar.copy(out=b1_all[:], in_=b1_bank[:])
+
+        def spread_biases():
+            b0_bank = flip_psum.tile([P, D2], F32, name="b0_bank", tag="bank")
+            for h in range(HALVES):
+                nc.tensor.transpose(
+                    out=b0_bank[:, h * P : (h + 1) * P],
+                    in_=b0_rows[:].bitcast(F32)[:, h : HALVES * P : HALVES],
+                    identity=ident[:],
+                )
+            nc.scalar.copy(
+                out=b0_cols[:].bitcast(F32).rearrange("q (j h) -> q j h", h=HALVES),
+                in_=b0_bank[:, 0 : HALVES * P].rearrange("q (h n) -> q n h", h=HALVES)[
+                    :, 0:PASSES_1, :
+                ],
+            )
+            b1_bank = flip_psum.tile([P, D2], F32, name="b1_bank", tag="bank")
+            nc.tensor.matmul(out=b1_bank[:], lhsT=ones[:], rhs=b1_rows[:], start=True, stop=True)
+            nc.scalar.copy(out=b1_all[:], in_=b1_bank[:])
 
         grouped_of = {}
         out_banks = {}
 
-        def front(c):
-            masked = stream.tile([P, CHUNK], BF16, name="masked")
-            for first, sets in pieces[c]:
-                cols = slice(first * K_PASS, (first + sets) * K_PASS)
-                as_read = "q (n h e) -> q h n e"
-                as_written = "q (h n e) -> q h n e"
-                nc.vector.tensor_mul(
-                    out=masked[:, cols].rearrange(as_written, h=HALVES, e=PAIR),
-                    in0=w_rows[c][:, cols].rearrange(as_read, h=HALVES, e=PAIR),
-                    in1=m_rows[c][:, cols].rearrange(as_read, h=HALVES, e=PAIR),
-                )
-                grouped_of[c, first] = flip(masked[:, cols], sets, True)
+        def front(i):
+            sets = PIECES[i][2]
+            masked = stream.tile([P, sets * K_PASS], BF16, name="masked")
+            as_read = "q (n h e) -> q h n e"
+            as_written = "q (h n e) -> q h n e"
+            nc.vector.tensor_mul(
+                out=masked[:].rearrange(as_written, h=HALVES, e=PAIR),
+                in0=w_rows[i][:].rearrange(as_read, h=HALVES, e=PAIR),
+                in1=m_rows[i][:].rearrange(as_read, h=HALVES, e=PAIR),
+            )
+            grouped_of[i] = flip(masked[:], sets, True)
 
-        def quantise(c):
-            for first, sets in pieces[c]:
-                cols = slice(first * P, (first + sets) * P)
-                nc.vector.quantize_mx(
-                    out=w_codes[:, c, cols].bitcast(FP8X4),
-                    scales=w_scales[:, c, cols],
-                    in_=grouped_of[c, first][:],
-                )
+        def quantise(i):
+            c, first, sets = PIECES[i]
+            cols = slice(first * P, (first + sets) * P)
+            nc.vector.quantize_mx(
+                out=w_codes[:, c, cols].bitcast(FP8X4),
+                scales=w_scales[:, c, cols],
+                in_=grouped_of[i][:],
+            )
 
-        def multiply_0(c):
-            h_bank = sum_psum.tile([P, SETS, P], F32, tag="sum")
-            for e in range(SETS):
+        def multiply_0(i):
+            c, first, sets = PIECES[i]
+            h_bank = sum_psum.tile([P, SETS, P], F32, name="h_bank", tag="sum")
+            for e in range(first, first + sets):
                 cols = slice(e * P, (e + 1) * P)
                 nc.tensor.matmul_mx(
                     out=h_bank[:, e, :],
@@ -161,7 +175,7 @@ def tile_patchedsparsenetwork_pa_s_kernel(tc, x, W0, b0, m0, W1, b1, m1, out):
                     start=True,
                     stop=True,
                 )
-            for e in range(SETS):
+            for e in range(first, first + sets):
                 pas, t = divmod(SETS * c + e, PACK)
                 nc.scalar.activation(
                     out=h_tiles[:, pas, t, :],
@@ -182,9 +196,11 @@ def tile_patchedsparsenetwork_pa_s_kernel(tc, x, W0, b0, m0, W1, b1, m1, out):
                 in_=h_grouped[:, pas, :, :].rearrange("q b t -> q (b t)"),
             )
 
-        def multiply_1(c):
-            out_banks[c] = sum_psum.tile([P, P], F32, name="out_bank", tag="sum")
-            for pas in range(PASSES_1):
+        def multiply_1(i):
+            c, first, sets = PIECES[i]
+            if first == 0:
+                out_banks[c] = sum_psum.tile([P, P], F32, name="out_bank", tag="sum")
+            for pas in range(first, first + sets):
                 cols = slice(pas * P, (pas + 1) * P)
                 nc.tensor.matmul_mx(
                     out=out_banks[c][:],
@@ -202,27 +218,31 @@ def tile_patchedsparsenetwork_pa_s_kernel(tc, x, W0, b0, m0, W1, b1, m1, out):
             nc.vector.tensor_scalar_max(out=out_sb[:, cols], in0=out_sb[:, cols], scalar1=0.0)
             nc.sync.dma_start(out=out[:, cols], in_=out_sb[:, cols])
 
-        layer_0 = range(CHUNKS_0)
-        layer_1 = range(CHUNKS_0, CHUNKS)
-        h_done = CHUNKS_0 - 1 + 2 * LAG
-        multiply_step = {c: max(c + LAG, h_done) for c in layer_1}
-        for i in range(CHUNKS + 2 * LAG):
-            if i < CHUNKS:
+        layer_0 = [i for i, piece in enumerate(PIECES) if piece[0] < CHUNKS_0]
+        layer_1 = [i for i, piece in enumerate(PIECES) if piece[0] >= CHUNKS_0]
+        h_done = layer_0[-1] + 2 * LAG
+        multiply_step = {i: max(i + LAG, h_done) for i in layer_1}
+        for i in range(len(PIECES) + 2 * LAG):
+            if i < len(PIECES):
                 front(i)
             if i == 0:
-                nc.vector.quantize_mx(
-                    out=x_codes[:].bitcast(FP8X4), scales=x_scales[:], in_=x_grouped[:]
-                )
-            if 0 <= i - LAG < CHUNKS:
+                x_grouped = flip_x()
+            if i == 1:
+                quantise_x(x_grouped)
+                spread_biases()
+            if 0 <= i - LAG < len(PIECES):
                 quantise(i - LAG)
-            if i - 2 * LAG in layer_0 and (i - 2 * LAG) % HALVES == HALVES - 1:
-                group_h((i - 2 * LAG) // HALVES)
-                quantise_h((i - 2 * LAG) // HALVES)
-            for c in layer_1:
-                if i == multiply_step[c] + LAG:
+            if i - 2 * LAG in layer_0:
+                c, first, sets = PIECES[i - 2 * LAG]
+                if (SETS * c + first + sets) % PACK == 0:
+                    group_h(c // HALVES)
+                    quantise_h(c // HALVES)
+            for j in layer_1:
+                c, first, sets = PIECES[j]
+                if i == multiply_step[j] + LAG and first + sets == SETS:
                     finish_out(c)
             if i - LAG in layer_0:
                 multiply_0(i - LAG)
-            for c in layer_1:
-                if i == multiply_step[c]:
-                    multiply_1(c)
+            for j in layer_1:
+                if i == multiply_step[j]:
+                    multiply_1(j)

@@ -51,6 +51,10 @@ def tile_patchedsparsenetwork_pa_s_kernel(tc, x, W0, b0, m0, W1, b1, m1, out):
         w_views += [W1.rearrange("(r q) k -> r q k", q=P)[r] for r in range(CHUNKS_1)]
         m_views += [m1.rearrange("(r q) k -> r q k", q=P)[r] for r in range(CHUNKS_1)]
         x_rows = consts.tile([P, D0], BF16)
+        b0_rows = consts.tile([P, K_PASS], BF16)
+        nc.vector.memset(b0_rows[:], 0.0)
+        b1_rows = consts.tile([P, D2], BF16)
+        nc.vector.memset(b1_rows[:], 0.0)
         w_rows, m_rows = [], []
         for i, (c, first, sets) in enumerate(PIECES):
             cols = slice(first * K_PASS, (first + sets) * K_PASS)
@@ -60,15 +64,11 @@ def tile_patchedsparsenetwork_pa_s_kernel(tc, x, W0, b0, m0, W1, b1, m1, out):
             nc.sync.dma_start(out=m_rows[i][:], in_=m_views[c][:, cols])
             if i == 0:
                 nc.sync.dma_start(out=x_rows[:], in_=x)
-
-        b0_rows = consts.tile([P, K_PASS], BF16)
-        nc.vector.memset(b0_rows[:], 0.0)
-        nc.gpsimd.dma_start(
-            out=b0_rows[0:PASSES_1, :], in_=b0.rearrange("(j n) -> j n", j=PASSES_1)
-        )
-        b1_rows = consts.tile([P, D2], BF16)
-        nc.vector.memset(b1_rows[:], 0.0)
-        nc.gpsimd.dma_start(out=b1_rows[0:1, :], in_=b1.rearrange("(o n) -> o n", o=1))
+            if i == 1:
+                nc.sync.dma_start(
+                    out=b0_rows[0:PASSES_1, :], in_=b0.rearrange("(j n) -> j n", j=PASSES_1)
+                )
+                nc.sync.dma_start(out=b1_rows[0:1, :], in_=b1.rearrange("(o n) -> o n", o=1))
 
         ident = consts.tile([P, P], F32)
         make_identity(nc, ident[:])
@@ -119,7 +119,7 @@ def tile_patchedsparsenetwork_pa_s_kernel(tc, x, W0, b0, m0, W1, b1, m1, out):
         b0_cols = consts.tile([P, PASSES_1 * PACK], BF16)
         b1_all = consts.tile([P, D2], F32)
 
-        def spread_biases():
+        def spread_b0():
             b0_bank = flip_psum.tile([P, D2], F32, name="b0_bank", tag="bank")
             for h in range(HALVES):
                 nc.tensor.transpose(
@@ -133,6 +133,8 @@ def tile_patchedsparsenetwork_pa_s_kernel(tc, x, W0, b0, m0, W1, b1, m1, out):
                     :, 0:PASSES_1, :
                 ],
             )
+
+        def spread_b1():
             b1_bank = flip_psum.tile([P, D2], F32, name="b1_bank", tag="bank")
             nc.tensor.matmul(out=b1_bank[:], lhsT=ones[:], rhs=b1_rows[:], start=True, stop=True)
             nc.scalar.copy(out=b1_all[:], in_=b1_bank[:])
@@ -185,7 +187,7 @@ def tile_patchedsparsenetwork_pa_s_kernel(tc, x, W0, b0, m0, W1, b1, m1, out):
                 )
 
         def group_h(pas):
-            nc.vector.tensor_copy(
+            nc.scalar.copy(
                 out=h_grouped[:, pas, :, :], in_=h_tiles[:, pas, :, :].rearrange("q t b -> q b t")
             )
 
@@ -215,7 +217,7 @@ def tile_patchedsparsenetwork_pa_s_kernel(tc, x, W0, b0, m0, W1, b1, m1, out):
         def finish_out(c):
             cols = slice((c - CHUNKS_0) * P, (c - CHUNKS_0 + 1) * P)
             nc.vector.tensor_add(out=out_sb[:, cols], in0=out_banks[c][:], in1=b1_all[:, cols])
-            nc.vector.tensor_scalar_max(out=out_sb[:, cols], in0=out_sb[:, cols], scalar1=0.0)
+            nc.scalar.activation(out=out_sb[:, cols], in_=out_sb[:, cols], func=RELU)
             nc.sync.dma_start(out=out[:, cols], in_=out_sb[:, cols])
 
         layer_0 = [i for i, piece in enumerate(PIECES) if piece[0] < CHUNKS_0]
@@ -227,15 +229,16 @@ def tile_patchedsparsenetwork_pa_s_kernel(tc, x, W0, b0, m0, W1, b1, m1, out):
                 front(i)
             if i == 0:
                 x_grouped = flip_x()
-            if i == 1:
+            if i == LAG:
                 quantise_x(x_grouped)
-                spread_biases()
+                spread_b0()
+            if i == layer_0[-1] + LAG + 1:
+                spread_b1()
             if 0 <= i - LAG < len(PIECES):
                 quantise(i - LAG)
             if i - 2 * LAG in layer_0:
                 c, first, sets = PIECES[i - 2 * LAG]
                 if (SETS * c + first + sets) % PACK == 0:
-                    group_h(c // HALVES)
                     quantise_h(c // HALVES)
             for j in layer_1:
                 c, first, sets = PIECES[j]
@@ -243,6 +246,9 @@ def tile_patchedsparsenetwork_pa_s_kernel(tc, x, W0, b0, m0, W1, b1, m1, out):
                     finish_out(c)
             if i - LAG in layer_0:
                 multiply_0(i - LAG)
+                c, first, sets = PIECES[i - LAG]
+                if (SETS * c + first + sets) % PACK == 0:
+                    group_h(c // HALVES)
             for j in layer_1:
                 if i == multiply_step[j]:
                     multiply_1(j)

@@ -187,7 +187,7 @@ def tile_patchedsparsenetwork_pa_s_kernel(tc, x, W0, b0, m0, W1, b1, m1, out):
                 )
 
         def group_h(pas):
-            nc.scalar.copy(
+            nc.vector.tensor_copy(
                 out=h_grouped[:, pas, :, :], in_=h_tiles[:, pas, :, :].rearrange("q t b -> q b t")
             )
 
@@ -217,7 +217,7 @@ def tile_patchedsparsenetwork_pa_s_kernel(tc, x, W0, b0, m0, W1, b1, m1, out):
         def finish_out(c):
             cols = slice((c - CHUNKS_0) * P, (c - CHUNKS_0 + 1) * P)
             nc.vector.tensor_add(out=out_sb[:, cols], in0=out_banks[c][:], in1=b1_all[:, cols])
-            nc.scalar.activation(out=out_sb[:, cols], in_=out_sb[:, cols], func=RELU)
+            nc.vector.tensor_scalar_max(out=out_sb[:, cols], in0=out_sb[:, cols], scalar1=0.0)
             nc.sync.dma_start(out=out[:, cols], in_=out_sb[:, cols])
 
         layer_0 = [i for i, piece in enumerate(PIECES) if piece[0] < CHUNKS_0]
@@ -234,21 +234,22 @@ def tile_patchedsparsenetwork_pa_s_kernel(tc, x, W0, b0, m0, W1, b1, m1, out):
                 spread_b0()
             if i == layer_0[-1] + LAG + 1:
                 spread_b1()
-            if 0 <= i - LAG < len(PIECES):
-                quantise(i - LAG)
+            h_pass = None
             if i - 2 * LAG in layer_0:
                 c, first, sets = PIECES[i - 2 * LAG]
                 if (SETS * c + first + sets) % PACK == 0:
-                    quantise_h(c // HALVES)
+                    h_pass = c // HALVES
+                    group_h(h_pass)
+            if 0 <= i - LAG < len(PIECES):
+                quantise(i - LAG)
+            if h_pass is not None:
+                quantise_h(h_pass)
             for j in layer_1:
                 c, first, sets = PIECES[j]
                 if i == multiply_step[j] + LAG and first + sets == SETS:
                     finish_out(c)
             if i - LAG in layer_0:
                 multiply_0(i - LAG)
-                c, first, sets = PIECES[i - LAG]
-                if (SETS * c + first + sets) % PACK == 0:
-                    group_h(c // HALVES)
             for j in layer_1:
                 if i == multiply_step[j]:
                     multiply_1(j)

@@ -18,18 +18,23 @@ HALVES = 2
 D0, D1, D2 = 512, 1024, 512
 FLOPS = 2 * P * (D0 * D1 + D1 * D2)
 
-SETS = 2
+SETS = 8
 PASSES_1 = D1 // K_PASS
-CHUNKS_0 = D1 // (P * SETS)
-CHUNKS_1 = D2 // P
-CHUNKS = CHUNKS_0 + CHUNKS_1
 LAG = 2
+W1_LAG = 3
+GROUP_LAG = 5
+H_LAG = 6
 
-CUT = (0, CHUNKS - 1)
+LOADS = [
+    *((tensor, s, 2) for s in range(0, SETS, 2) for tensor in (0, 1)),
+    *((tensor, s, 2) for s in range(0, SETS - 2, 2) for tensor in (2, 3)),
+    (2, SETS - 2, 2),
+    *((3, s, 1) for s in (SETS - 2, SETS - 1)),
+]
 PIECES = [
-    (c, first, 1 if c in CUT else SETS)
-    for c in range(CHUNKS)
-    for first in (range(SETS) if c in CUT else (0,))
+    *((0, s, 2) for s in range(0, SETS, 2)),
+    *((1, s, 2) for s in range(0, SETS - 2, 2)),
+    *((1, s, 1) for s in (SETS - 2, SETS - 1)),
 ]
 
 
@@ -39,32 +44,32 @@ def tile_patchedsparsenetwork_pa_s_kernel(tc, x, W0, b0, m0, W1, b1, m1, out):
         ctx.enter_context(tc.manual_schedule())
         consts = ctx.enter_context(tc.tile_pool(name="consts", bufs=1))
         keep = ctx.enter_context(tc.tile_pool(name="keep", bufs=1))
-        stream = ctx.enter_context(tc.tile_pool(name="stream", bufs=len(PIECES)))
+        loads = ctx.enter_context(tc.tile_pool(name="loads", bufs=len(LOADS)))
+        stream = ctx.enter_context(tc.tile_pool(name="stream", bufs=len(PIECES) + 1))
         flip_psum = ctx.enter_context(tc.psum_pool(name="flip_psum", bufs=4))
         sum_psum = ctx.enter_context(tc.psum_pool(name="sum_psum", bufs=4))
 
-        deal = "(g q j e) k -> g j q (e k)"
-        w_dealt = W0.rearrange(deal, g=PASSES_1, q=P, e=SETS)
-        m_dealt = m0.rearrange(deal, g=PASSES_1, q=P, e=SETS)
-        w_views = [w_dealt[c // 2, c % 2] for c in range(CHUNKS_0)]
-        m_views = [m_dealt[c // 2, c % 2] for c in range(CHUNKS_0)]
-        w_views += [W1.rearrange("(r q) k -> r q k", q=P)[r] for r in range(CHUNKS_1)]
-        m_views += [m1.rearrange("(r q) k -> r q k", q=P)[r] for r in range(CHUNKS_1)]
         x_rows = consts.tile([P, D0], BF16)
         b0_rows = consts.tile([P, K_PASS], BF16)
         nc.vector.memset(b0_rows[:], 0.0)
         b1_rows = consts.tile([P, D2], BF16)
         nc.vector.memset(b1_rows[:], 0.0)
-        w_rows, m_rows = [], []
-        for i, (c, first, sets) in enumerate(PIECES):
-            cols = slice(first * K_PASS, (first + sets) * K_PASS)
-            w_rows.append(stream.tile([P, sets * K_PASS], BF16, name="w_rows"))
-            m_rows.append(stream.tile([P, sets * K_PASS], BF16, name="m_rows"))
-            nc.sync.dma_start(out=w_rows[i][:], in_=w_views[c][:, cols])
-            nc.sync.dma_start(out=m_rows[i][:], in_=m_views[c][:, cols])
-            if i == 0:
-                nc.sync.dma_start(out=x_rows[:], in_=x)
+        loaded = {}
+        tensors = (W0, m0, W1, m1)
+        for i, (number, first, sets) in enumerate(LOADS):
+            if number < 2:
+                rows = tensors[number].rearrange("(g q t) k -> g q (t k)", q=P, t=PACK)
+                run, start = rows[first // PACK], first % PACK
+            else:
+                rows = tensors[number].rearrange("(r q) k -> r q k", q=P)
+                run, start = rows[first // PASSES_1], first % PASSES_1
+            tile = loads.tile([P, sets * K_PASS], BF16, name="load")
+            nc.sync.dma_start(out=tile[:], in_=run[:, start * K_PASS : (start + sets) * K_PASS])
+            for s in range(sets):
+                loaded[number, first + s] = (tile, s)
             if i == 1:
+                nc.sync.dma_start(out=x_rows[:], in_=x)
+            if i == 3:
                 nc.sync.dma_start(
                     out=b0_rows[0:PASSES_1, :], in_=b0.rearrange("(j n) -> j n", j=PASSES_1)
                 )
@@ -77,8 +82,8 @@ def tile_patchedsparsenetwork_pa_s_kernel(tc, x, W0, b0, m0, W1, b1, m1, out):
 
         x_codes = keep.tile([P, P], U32, align_bytes=64)
         x_scales = keep.tile([P, P], U8, align_bytes=64)
-        w_codes = keep.tile([P, CHUNKS, SETS * P], U32, align_bytes=64)
-        w_scales = keep.tile([P, CHUNKS, SETS * P], U8, align_bytes=64)
+        w_codes = keep.tile([P, 2, SETS * P], U32, align_bytes=64)
+        w_scales = keep.tile([P, 2, SETS * P], U8, align_bytes=64)
         h_codes = keep.tile([P, PASSES_1, P], U32, align_bytes=64)
         h_scales = keep.tile([P, PASSES_1, P], U8, align_bytes=64)
         h_tiles = keep.tile([P, PASSES_1, PACK, P], BF16)
@@ -143,47 +148,51 @@ def tile_patchedsparsenetwork_pa_s_kernel(tc, x, W0, b0, m0, W1, b1, m1, out):
         out_banks = {}
 
         def front(i):
-            sets = PIECES[i][2]
+            layer, first, sets = PIECES[i]
+            sides = []
+            for number in (2 * layer, 2 * layer + 1):
+                tile, s = loaded[number, first]
+                sides.append(tile[:, s * K_PASS : (s + sets) * K_PASS])
             masked = stream.tile([P, sets * K_PASS], BF16, name="masked")
             as_read = "q (n h e) -> q h n e"
             as_written = "q (h n e) -> q h n e"
             nc.vector.tensor_mul(
                 out=masked[:].rearrange(as_written, h=HALVES, e=PAIR),
-                in0=w_rows[i][:].rearrange(as_read, h=HALVES, e=PAIR),
-                in1=m_rows[i][:].rearrange(as_read, h=HALVES, e=PAIR),
+                in0=sides[0].rearrange(as_read, h=HALVES, e=PAIR),
+                in1=sides[1].rearrange(as_read, h=HALVES, e=PAIR),
             )
             grouped_of[i] = flip(masked[:], sets, True)
 
         def quantise(i):
-            c, first, sets = PIECES[i]
+            layer, first, sets = PIECES[i]
             cols = slice(first * P, (first + sets) * P)
             nc.vector.quantize_mx(
-                out=w_codes[:, c, cols].bitcast(FP8X4),
-                scales=w_scales[:, c, cols],
+                out=w_codes[:, layer, cols].bitcast(FP8X4),
+                scales=w_scales[:, layer, cols],
                 in_=grouped_of[i][:],
             )
 
         def multiply_0(i):
-            c, first, sets = PIECES[i]
-            h_bank = sum_psum.tile([P, SETS, P], F32, name="h_bank", tag="sum")
-            for e in range(first, first + sets):
-                cols = slice(e * P, (e + 1) * P)
+            layer, first, sets = PIECES[i]
+            h_bank = sum_psum.tile([P, sets, P], F32, name="h_bank", tag="sum")
+            for s in range(sets):
+                cols = slice((first + s) * P, (first + s + 1) * P)
                 nc.tensor.matmul_mx(
-                    out=h_bank[:, e, :],
-                    lhsT=w_codes[:, c, cols].bitcast(FP8X4),
-                    lhsT_scale=w_scales[:, c, cols],
+                    out=h_bank[:, s, :],
+                    lhsT=w_codes[:, 0, cols].bitcast(FP8X4),
+                    lhsT_scale=w_scales[:, 0, cols],
                     rhs=x_codes[:].bitcast(FP8X4),
                     rhs_scale=x_scales[:],
                     start=True,
                     stop=True,
                 )
-            for e in range(first, first + sets):
-                pas, t = divmod(SETS * c + e, PACK)
+            for s in range(sets):
+                pas, t = divmod(first + s, PACK)
                 nc.scalar.activation(
                     out=h_tiles[:, pas, t, :],
-                    in_=h_bank[:, e, :],
+                    in_=h_bank[:, s, :],
                     func=RELU,
-                    bias=b0_cols[:, SETS * c + e : SETS * c + e + 1],
+                    bias=b0_cols[:, first + s : first + s + 1],
                 )
 
         def group_h(pas):
@@ -199,57 +208,64 @@ def tile_patchedsparsenetwork_pa_s_kernel(tc, x, W0, b0, m0, W1, b1, m1, out):
             )
 
         def multiply_1(i):
-            c, first, sets = PIECES[i]
-            if first == 0:
-                out_banks[c] = sum_psum.tile([P, P], F32, name="out_bank", tag="sum")
-            for pas in range(first, first + sets):
-                cols = slice(pas * P, (pas + 1) * P)
+            layer, first, sets = PIECES[i]
+            for s in range(first, first + sets):
+                r, pas = divmod(s, PASSES_1)
+                if pas == 0:
+                    out_banks[r] = sum_psum.tile([P, P], F32, name="out_bank", tag="sum")
+                cols = slice(s * P, (s + 1) * P)
                 nc.tensor.matmul_mx(
-                    out=out_banks[c][:],
+                    out=out_banks[r][:],
                     lhsT=h_codes[:, pas, :].bitcast(FP8X4),
                     lhsT_scale=h_scales[:, pas, :],
-                    rhs=w_codes[:, c, cols].bitcast(FP8X4),
-                    rhs_scale=w_scales[:, c, cols],
+                    rhs=w_codes[:, 1, cols].bitcast(FP8X4),
+                    rhs_scale=w_scales[:, 1, cols],
                     start=(pas == 0),
                     stop=(pas == PASSES_1 - 1),
                 )
 
-        def finish_out(c):
-            cols = slice((c - CHUNKS_0) * P, (c - CHUNKS_0 + 1) * P)
-            nc.vector.tensor_add(out=out_sb[:, cols], in0=out_banks[c][:], in1=b1_all[:, cols])
-            nc.vector.tensor_scalar_max(out=out_sb[:, cols], in0=out_sb[:, cols], scalar1=0.0)
+        def finish_out(r):
+            cols = slice(r * P, (r + 1) * P)
+            nc.vector.tensor_add(out=out_sb[:, cols], in0=out_banks[r][:], in1=b1_all[:, cols])
+            if r < D2 // P - 1:
+                nc.scalar.activation(out=out_sb[:, cols], in_=out_sb[:, cols], func=RELU)
+            else:
+                nc.vector.tensor_scalar_max(out=out_sb[:, cols], in0=out_sb[:, cols], scalar1=0.0)
             nc.sync.dma_start(out=out[:, cols], in_=out_sb[:, cols])
 
-        layer_0 = [i for i, piece in enumerate(PIECES) if piece[0] < CHUNKS_0]
-        layer_1 = [i for i, piece in enumerate(PIECES) if piece[0] >= CHUNKS_0]
-        h_done = layer_0[-1] + 2 * LAG
-        multiply_step = {i: max(i + LAG, h_done) for i in layer_1}
-        for i in range(len(PIECES) + 2 * LAG):
-            if i < len(PIECES):
-                front(i)
+        layer_0 = [i for i, piece in enumerate(PIECES) if piece[0] == 0]
+        layer_1 = [i for i, piece in enumerate(PIECES) if piece[0] == 1]
+        quantise_step = {i: i + (LAG if i in layer_0 else W1_LAG) for i in range(len(PIECES))}
+        completes = {
+            sum(PIECES[i][1:]) // PACK - 1: i for i in layer_0 if sum(PIECES[i][1:]) % PACK == 0
+        }
+        h_done = layer_0[-1] + H_LAG
+        multiply_step = {i: max(quantise_step[i], h_done) for i in layer_1}
+        for i in range(len(PIECES) + W1_LAG + LAG):
             if i == 0:
                 x_grouped = flip_x()
-            if i == LAG:
+            if i < len(PIECES):
+                front(i)
+            for pas in completes:
+                if i == completes[pas] + GROUP_LAG:
+                    group_h(pas)
+            if i == 1:
                 quantise_x(x_grouped)
                 spread_b0()
-            if i == layer_0[-1] + LAG + 1:
                 spread_b1()
-            h_pass = None
-            if i - 2 * LAG in layer_0:
-                c, first, sets = PIECES[i - 2 * LAG]
-                if (SETS * c + first + sets) % PACK == 0:
-                    h_pass = c // HALVES
-                    group_h(h_pass)
-            if 0 <= i - LAG < len(PIECES):
-                quantise(i - LAG)
-            if h_pass is not None:
-                quantise_h(h_pass)
+            for pas in completes:
+                if i == completes[pas] + H_LAG:
+                    quantise_h(pas)
+            for j in quantise_step:
+                if i == quantise_step[j]:
+                    quantise(j)
             for j in layer_1:
-                c, first, sets = PIECES[j]
-                if i == multiply_step[j] + LAG and first + sets == SETS:
-                    finish_out(c)
-            if i - LAG in layer_0:
-                multiply_0(i - LAG)
+                r, pas = divmod(sum(PIECES[j][1:]) - 1, PASSES_1)
+                if i == multiply_step[j] + LAG and pas == PASSES_1 - 1:
+                    finish_out(r)
+            for j in layer_0:
+                if i == quantise_step[j]:
+                    multiply_0(j)
             for j in layer_1:
                 if i == multiply_step[j]:
                     multiply_1(j)

from contextlib import ExitStack

import concourse.mybir as mybir
from concourse.masks import make_identity

BF16 = mybir.dt.bfloat16
F32 = mybir.dt.float32
U32 = mybir.dt.uint32
U8 = mybir.dt.uint8
FP8X4 = mybir.dt.float8_e4m3fn_x4
RELU = mybir.ActivationFunctionType.Relu

P = 128
PAIR = 2
PACK = 4
K_PASS = P * PACK
HALVES = 2
D0, D1, D2 = 512, 1024, 512
FLOPS = 2 * P * (D0 * D1 + D1 * D2)

SETS = 8
PASSES_1 = D1 // K_PASS
LAG = 2
W1_LAG = 3
GROUP_LAG = 5
H_LAG = 6

LOADS = [
    *((tensor, s, 2) for s in range(0, SETS, 2) for tensor in (0, 1)),
    *((tensor, s, 2) for s in range(0, SETS - 2, 2) for tensor in (2, 3)),
    (2, SETS - 2, 2),
    *((3, s, 1) for s in (SETS - 2, SETS - 1)),
]
PIECES = [
    *((0, s, 2) for s in range(0, SETS, 2)),
    *((1, s, 2) for s in range(0, SETS - 2, 2)),
    *((1, s, 1) for s in (SETS - 2, SETS - 1)),
]


def tile_patchedsparsenetwork_pa_s_kernel(tc, x, W0, b0, m0, W1, b1, m1, out):
    nc = tc.nc
    with ExitStack() as ctx:
        ctx.enter_context(tc.manual_schedule())
        consts = ctx.enter_context(tc.tile_pool(name="consts", bufs=1))
        keep = ctx.enter_context(tc.tile_pool(name="keep", bufs=1))
        loads = ctx.enter_context(tc.tile_pool(name="loads", bufs=len(LOADS)))
        stream = ctx.enter_context(tc.tile_pool(name="stream", bufs=len(PIECES) + 1))
        flip_psum = ctx.enter_context(tc.psum_pool(name="flip_psum", bufs=4))
        sum_psum = ctx.enter_context(tc.psum_pool(name="sum_psum", bufs=4))

        x_rows = consts.tile([P, D0], BF16)
        b0_rows = consts.tile([P, K_PASS], BF16)
        nc.vector.memset(b0_rows[:], 0.0)
        b1_rows = consts.tile([P, D2], BF16)
        nc.vector.memset(b1_rows[:], 0.0)
        loaded = {}
        tensors = (W0, m0, W1, m1)
        for i, (number, first, sets) in enumerate(LOADS):
            if number < 2:
                rows = tensors[number].rearrange("(g q t) k -> g q (t k)", q=P, t=PACK)
                run, start = rows[first // PACK], first % PACK
            else:
                rows = tensors[number].rearrange("(r q) k -> r q k", q=P)
                run, start = rows[first // PASSES_1], first % PASSES_1
            tile = loads.tile([P, sets * K_PASS], BF16, name="load")
            nc.sync.dma_start(out=tile[:], in_=run[:, start * K_PASS : (start + sets) * K_PASS])
            for s in range(sets):
                loaded[number, first + s] = (tile, s)
            if i == 1:
                nc.sync.dma_start(out=x_rows[:], in_=x)
            if i == 3:
                nc.sync.dma_start(
                    out=b0_rows[0:PASSES_1, :], in_=b0.rearrange("(j n) -> j n", j=PASSES_1)
                )
                nc.sync.dma_start(out=b1_rows[0:1, :], in_=b1.rearrange("(o n) -> o n", o=1))

        ident = consts.tile([P, P], F32)
        make_identity(nc, ident[:])
        ones = consts.tile([P, P], BF16)
        nc.vector.memset(ones[:], 1.0)

        x_codes = keep.tile([P, P], U32, align_bytes=64)
        x_scales = keep.tile([P, P], U8, align_bytes=64)
        w_codes = keep.tile([P, 2, SETS * P], U32, align_bytes=64)
        w_scales = keep.tile([P, 2, SETS * P], U8, align_bytes=64)
        h_codes = keep.tile([P, PASSES_1, P], U32, align_bytes=64)
        h_scales = keep.tile([P, PASSES_1, P], U8, align_bytes=64)
        h_tiles = keep.tile([P, PASSES_1, PACK, P], BF16)
        h_grouped = keep.tile([P, PASSES_1, P, PACK], BF16, align_bytes=64)
        out_sb = keep.tile([P, D2], F32)

        def flip(rows, sets, parted):
            words = rows.bitcast(F32)
            bank = flip_psum.tile([P, D2], F32, tag="bank")
            for block in range(sets * HALVES):
                s, h = divmod(block, HALVES)
                if parted:
                    in_cols = slice((h * sets + s) * P, (h * sets + s + 1) * P)
                else:
                    in_cols = slice(s * HALVES * P + h, (s + 1) * HALVES * P, HALVES)
                nc.tensor.transpose(
                    out=bank[:, block * P : (block + 1) * P],
                    in_=words[:, in_cols],
                    identity=ident[:],
                )
            grouped = stream.tile([P, sets * P * PACK], BF16, name="grouped", align_bytes=64)
            nc.scalar.copy(
                out=grouped[:].bitcast(F32).rearrange("q (s n h) -> q s n h", s=sets, h=HALVES),
                in_=bank[:, 0 : sets * HALVES * P].rearrange(
                    "q (s h n) -> q s n h", s=sets, h=HALVES
                ),
            )
            return grouped

        def flip_x():
            return flip(x_rows[:], 1, False)

        def quantise_x(x_grouped):
            nc.vector.quantize_mx(
                out=x_codes[:].bitcast(FP8X4), scales=x_scales[:], in_=x_grouped[:]
            )

        b0_cols = consts.tile([P, PASSES_1 * PACK], BF16)
        b1_all = consts.tile([P, D2], F32)

        def spread_b0():
            b0_bank = flip_psum.tile([P, D2], F32, name="b0_bank", tag="bank")
            for h in range(HALVES):
                nc.tensor.transpose(
                    out=b0_bank[:, h * P : (h + 1) * P],
                    in_=b0_rows[:].bitcast(F32)[:, h : HALVES * P : HALVES],
                    identity=ident[:],
                )
            nc.scalar.copy(
                out=b0_cols[:].bitcast(F32).rearrange("q (j h) -> q j h", h=HALVES),
                in_=b0_bank[:, 0 : HALVES * P].rearrange("q (h n) -> q n h", h=HALVES)[
                    :, 0:PASSES_1, :
                ],
            )

        def spread_b1():
            b1_bank = flip_psum.tile([P, D2], F32, name="b1_bank", tag="bank")
            nc.tensor.matmul(out=b1_bank[:], lhsT=ones[:], rhs=b1_rows[:], start=True, stop=True)
            nc.scalar.copy(out=b1_all[:], in_=b1_bank[:])

        grouped_of = {}
        out_banks = {}

        def front(i):
            layer, first, sets = PIECES[i]
            sides = []
            for number in (2 * layer, 2 * layer + 1):
                tile, s = loaded[number, first]
                sides.append(tile[:, s * K_PASS : (s + sets) * K_PASS])
            masked = stream.tile([P, sets * K_PASS], BF16, name="masked")
            as_read = "q (n h e) -> q h n e"
            as_written = "q (h n e) -> q h n e"
            nc.vector.tensor_mul(
                out=masked[:].rearrange(as_written, h=HALVES, e=PAIR),
                in0=sides[0].rearrange(as_read, h=HALVES, e=PAIR),
                in1=sides[1].rearrange(as_read, h=HALVES, e=PAIR),
            )
            grouped_of[i] = flip(masked[:], sets, True)

        def quantise(i):
            layer, first, sets = PIECES[i]
            cols = slice(first * P, (first + sets) * P)
            nc.vector.quantize_mx(
                out=w_codes[:, layer, cols].bitcast(FP8X4),
                scales=w_scales[:, layer, cols],
                in_=grouped_of[i][:],
            )

        def multiply_0(i):
            layer, first, sets = PIECES[i]
            h_bank = sum_psum.tile([P, sets, P], F32, name="h_bank", tag="sum")
            for s in range(sets):
                cols = slice((first + s) * P, (first + s + 1) * P)
                nc.tensor.matmul_mx(
                    out=h_bank[:, s, :],
                    lhsT=w_codes[:, 0, cols].bitcast(FP8X4),
                    lhsT_scale=w_scales[:, 0, cols],
                    rhs=x_codes[:].bitcast(FP8X4),
                    rhs_scale=x_scales[:],
                    start=True,
                    stop=True,
                )
            for s in range(sets):
                pas, t = divmod(first + s, PACK)
                nc.scalar.activation(
                    out=h_tiles[:, pas, t, :],
                    in_=h_bank[:, s, :],
                    func=RELU,
                    bias=b0_cols[:, first + s : first + s + 1],
                )

        def group_h(pas):
            nc.vector.tensor_copy(
                out=h_grouped[:, pas, :, :], in_=h_tiles[:, pas, :, :].rearrange("q t b -> q b t")
            )

        def quantise_h(pas):
            nc.vector.quantize_mx(
                out=h_codes[:, pas, :].bitcast(FP8X4),
                scales=h_scales[:, pas, :],
                in_=h_grouped[:, pas, :, :].rearrange("q b t -> q (b t)"),
            )

        def multiply_1(i):
            layer, first, sets = PIECES[i]
            for s in range(first, first + sets):
                r, pas = divmod(s, PASSES_1)
                if pas == 0:
                    out_banks[r] = sum_psum.tile([P, P], F32, name="out_bank", tag="sum")
                cols = slice(s * P, (s + 1) * P)
                nc.tensor.matmul_mx(
                    out=out_banks[r][:],
                    lhsT=h_codes[:, pas, :].bitcast(FP8X4),
                    lhsT_scale=h_scales[:, pas, :],
                    rhs=w_codes[:, 1, cols].bitcast(FP8X4),
                    rhs_scale=w_scales[:, 1, cols],
                    start=(pas == 0),
                    stop=(pas == PASSES_1 - 1),
                )

        def finish_out(r):
            cols = slice(r * P, (r + 1) * P)
            nc.vector.tensor_add(out=out_sb[:, cols], in0=out_banks[r][:], in1=b1_all[:, cols])
            if r < D2 // P - 1:
                nc.scalar.activation(out=out_sb[:, cols], in_=out_sb[:, cols], func=RELU)
            else:
                nc.vector.tensor_scalar_max(out=out_sb[:, cols], in0=out_sb[:, cols], scalar1=0.0)
            nc.sync.dma_start(out=out[:, cols], in_=out_sb[:, cols])

        layer_0 = [i for i, piece in enumerate(PIECES) if piece[0] == 0]
        layer_1 = [i for i, piece in enumerate(PIECES) if piece[0] == 1]
        quantise_step = {i: i + (LAG if i in layer_0 else W1_LAG) for i in range(len(PIECES))}
        completes = {
            sum(PIECES[i][1:]) // PACK - 1: i for i in layer_0 if sum(PIECES[i][1:]) % PACK == 0
        }
        h_done = layer_0[-1] + H_LAG
        multiply_step = {i: max(quantise_step[i], h_done) for i in layer_1}
        for i in range(len(PIECES) + W1_LAG + LAG):
            if i == 0:
                x_grouped = flip_x()
            if i < len(PIECES):
                front(i)
            for pas in completes:
                if i == completes[pas] + GROUP_LAG:
                    group_h(pas)
            if i == 1:
                quantise_x(x_grouped)
                spread_b0()
                spread_b1()
            for pas in completes:
                if i == completes[pas] + H_LAG:
                    quantise_h(pas)
            for j in quantise_step:
                if i == quantise_step[j]:
                    quantise(j)
            for j in layer_1:
                r, pas = divmod(sum(PIECES[j][1:]) - 1, PASSES_1)
                if i == multiply_step[j] + LAG and pas == PASSES_1 - 1:
                    finish_out(r)
            for j in layer_0:
                if i == quantise_step[j]:
                    multiply_0(j)
            for j in layer_1:
                if i == multiply_step[j]:
                    multiply_1(j)
